import numpy as np
import ml_dtypes


def mxq(x, axis, fmt="e4m3"):
    dtype, down = {"e4m3": (ml_dtypes.float8_e4m3fn, 7), "e5m2": (ml_dtypes.float8_e5m2, 14)}[fmt]
    v = np.moveaxis(np.asarray(x, np.float32).astype(ml_dtypes.bfloat16).astype(np.float64), axis, -1)
    blocks = v.reshape(v.shape[:-1] + (-1, 32))
    amax = np.abs(blocks).max(-1, keepdims=True)
    byte = np.maximum(np.where(amax > 0, np.frexp(amax)[1] - 1 + 127, 0) - down, 1)
    scale = np.exp2(byte - 127.0)
    codes = (blocks / scale).astype(np.float32).astype(dtype).astype(np.float64)
    return np.moveaxis((codes * scale).reshape(v.shape), -1, axis)


WIDE = False


def mx_kscale(k):
    if not WIDE:
        return np.ones(k)
    levels = np.array([10, -10, 5, -5, 0])
    a = np.random.permutation(np.resize(levels, k // 512 * 4)).reshape(k // 512, 4)
    idx = np.arange(k)
    return np.exp2(a[idx // 512, idx % 128 // 32])


BF16 = ml_dtypes.bfloat16


def bf(x):
    return np.asarray(x, np.float32).astype(BF16)


def f64(x):
    return np.asarray(x).astype(np.float64)


B, S, E, H, D, XL, TOPK = 2, 128, 8192, 8, 64, 512, 8
HD = H * D


def l2norm(x):
    return x / np.maximum(np.sqrt((x * x).sum(-1, keepdims=True)), 1e-12)


def split_heads(x):
    return x.reshape(B, S, H, D).transpose(0, 2, 1, 3)


def setup_inputs():
    n = np.random.standard_normal
    s = mx_kscale(E)
    return {"input": bf(n((B, S, E)) * s),
            "Wq": bf(n((HD, E)) / np.sqrt(E) / s), "bq": bf(n(HD) * 0.1),
            "Wk": bf(n((HD, E)) / np.sqrt(E) / s), "bk": bf(n(HD) * 0.1),
            "Wv": bf(n((HD, E)) / np.sqrt(E) / s), "bv": bf(n(HD) * 0.1)}


def reference(input, Wq, bq, Wk, bk, Wv, bv):
    xq = mxq(f64(input), 2, "e4m3")
    q = split_heads(l2norm((xq @ mxq(f64(Wq), 1, "e4m3").T) + f64(bq)))
    k = split_heads(l2norm((xq @ mxq(f64(Wk), 1, "e4m3").T) + f64(bk)))
    v = split_heads((xq @ mxq(f64(Wv), 1, "e4m3").T) + f64(bv))
    return q, k, v

@@ -1,0 +1,248 @@
+from contextlib import ExitStack
+
+import concourse.mybir as mybir
+from concourse.masks import make_identity
+
+F32 = mybir.dt.float32
+BF16 = mybir.dt.bfloat16
+U32 = mybir.dt.uint32
+U8 = mybir.dt.uint8
+FP8X4 = mybir.dt.float8_e4m3fn_x4
+ADD = mybir.AluOpType.add
+SQUARE = mybir.ActivationFunctionType.Square
+SQRT = mybir.ActivationFunctionType.Sqrt
+COPY = mybir.ActivationFunctionType.Copy
+
+P = 128
+K = 8192
+K_PASS = 512
+WORDS_PASS = K_PASS // 2
+PASSES = K // K_PASS
+TOKEN_TILES = 2
+FEATURES = 512
+FEATURE_TILES = FEATURES // P
+HEADS = 8
+WEIGHTS = 3
+
+ROUND_PASSES = 4
+K_ROUND = ROUND_PASSES * K_PASS
+ROUNDS_PER_WEIGHT = PASSES // ROUND_PASSES
+ROUNDS = WEIGHTS * ROUNDS_PER_WEIGHT
+LAG = 2
+LOADS_AHEAD = 5
+
+UNIT_COLUMNS = 512
+BANK_COLUMNS = UNIT_COLUMNS // 2
+
+FLOPS = 2 * TOKEN_TILES * P * WEIGHTS * FEATURES * K
+
+
+def tile_knnxlmultiheadsattention_pa_k_kernel(
+    tc, x, wq, bq, wk, bk, wv, bv, out_q, out_k, out_v
+):
+    nc = tc.nc
+    weights = [wq, wk, wv]
+    biases = [bq, bk, bv]
+    outs = [out_q, out_k, out_v]
+
+    with ExitStack() as ctx:
+        ctx.enter_context(tc.manual_schedule())
+        const = ctx.enter_context(tc.tile_pool(name="const", bufs=1))
+        x_raw_pool = ctx.enter_context(tc.tile_pool(name="x_raw", bufs=ROUNDS_PER_WEIGHT))
+        w_raw_pool = ctx.enter_context(tc.tile_pool(name="w_raw", bufs=LOADS_AHEAD))
+        grouped_pool = ctx.enter_context(tc.tile_pool(name="grouped", bufs=4))
+        w_mx_pool = ctx.enter_context(tc.tile_pool(name="w_mx", bufs=3))
+        result_pool = ctx.enter_context(tc.tile_pool(name="result", bufs=4))
+        small_pool = ctx.enter_context(tc.tile_pool(name="small", bufs=4))
+        sum_pool = ctx.enter_context(tc.psum_pool(name="sums", bufs=3))
+        bank_pool = ctx.enter_context(tc.psum_pool(name="banks", bufs=5))
+
+        x_by_token = x.rearrange("b s k -> s b k")
+        x_words = {}
+        w_words = {}
+
+        def load_x(c):
+            x_raw = x_raw_pool.tile([P, TOKEN_TILES * K_ROUND], BF16)
+            nc.sync.dma_start(
+                out=x_raw[:].rearrange("p (t k) -> p t k", t=TOKEN_TILES),
+                in_=x_by_token[:, :, c * K_ROUND : (c + 1) * K_ROUND],
+            )
+            x_words[c] = x_raw[:].bitcast(F32).rearrange("p (t w) -> p t w", t=TOKEN_TILES)
+
+        def load_w(r):
+            w, c = divmod(r, ROUNDS_PER_WEIGHT)
+            w_raw = w_raw_pool.tile([P, FEATURE_TILES * K_ROUND], BF16)
+            nc.sync.dma_start(
+                out=w_raw[:].rearrange("p (f k) -> p f k", f=FEATURE_TILES),
+                in_=weights[w].rearrange("(f p) k -> p f k", p=P)[
+                    :, :, c * K_ROUND : (c + 1) * K_ROUND
+                ],
+            )
+            w_words[r] = w_raw[:].bitcast(F32).rearrange("p (f w) -> p f w", f=FEATURE_TILES)
+
+        for r in range(LOADS_AHEAD):
+            if r < ROUNDS_PER_WEIGHT:
+                load_x(r)
+            load_w(r)
+
+        identity = const.tile([P, P], F32)
+        make_identity(nc, identity[:])
+
+        warm = const.tile([P, 1], F32)
+        nc.vector.memset(warm[:], 1.0)
+        nc.scalar.activation(out=warm[:], in_=warm[:], func=SQRT)
+
+        bias_rows = const.tile([P, WEIGHTS * FEATURES], BF16)
+        nc.vector.memset(bias_rows[:], 0.0)
+        ones = const.tile([P, P], BF16)
+        nc.vector.memset(ones[:], 1.0)
+        bias_all = const.tile([P, WEIGHTS * FEATURES], F32)
+        for w in range(WEIGHTS):
+            columns = slice(w * FEATURES, (w + 1) * FEATURES)
+            nc.scalar.dma_start(
+                out=bias_rows[0:1, columns], in_=biases[w].rearrange("(o n) -> o n", o=1)
+            )
+            bank = bank_pool.tile([P, 2, BANK_COLUMNS], F32)
+            spread = bank[:].rearrange("p u n -> p (u n)")
+            nc.tensor.matmul(spread, lhsT=ones[:], rhs=bias_rows[:, columns], start=True, stop=True)
+            nc.vector.tensor_copy(out=bias_all[:, columns], in_=spread)
+
+        x_codes = const.tile([P, PASSES * TOKEN_TILES * P], U32, align_bytes=64)
+        x_scales = const.tile([P, PASSES * TOKEN_TILES * P], U8, align_bytes=64)
+
+        def prepare_unit(sources, codes, scales, vector_helps):
+            grouped = grouped_pool.tile([P, 4 * UNIT_COLUMNS], BF16, align_bytes=64)
+            grouped_words = grouped[:].bitcast(F32).rearrange("p (n u) -> p n u", u=2)
+            for half in range(2):
+                bank = bank_pool.tile([P, 2, BANK_COLUMNS], F32)
+                for j in range(2):
+                    for u in range(2):
+                        nc.tensor.transpose(
+                            bank[:, u, j * P : (j + 1) * P],
+                            sources[2 * half + j][:, u * P : (u + 1) * P],
+                            identity[:],
+                        )
+                side_by_side = grouped_words[:, half * BANK_COLUMNS : (half + 1) * BANK_COLUMNS, :]
+                alternately = bank[:].rearrange("p u n -> p n u")
+                if vector_helps and half == 0:
+                    nc.vector.tensor_copy(out=side_by_side, in_=alternately)
+                else:
+                    nc.scalar.copy(out=side_by_side, in_=alternately)
+            nc.vector.quantize_mx(out=codes.bitcast(FP8X4), scales=scales, in_=grouped[:])
+
+        def prepare_x(c):
+            for i in range(0, ROUND_PASSES, 2):
+                g = c * ROUND_PASSES + i
+                columns = slice(g * TOKEN_TILES * P, (g + 2) * TOKEN_TILES * P)
+                prepare_unit(
+                    [
+                        x_words[c][:, t, (i + d) * WORDS_PASS : (i + d + 1) * WORDS_PASS]
+                        for d in range(2)
+                        for t in range(TOKEN_TILES)
+                    ],
+                    x_codes[:, columns],
+                    x_scales[:, columns],
+                    vector_helps=(i % 4 == 0),
+                )
+
+        w_codes = {}
+        w_scales = {}
+
+        def prepare_w(r):
+            codes = w_mx_pool.tile([P, ROUND_PASSES * FEATURES], U32, align_bytes=64)
+            scales = w_mx_pool.tile([P, ROUND_PASSES * FEATURES], U8, align_bytes=64)
+            w_codes[r] = codes
+            w_scales[r] = scales
+            for i in range(ROUND_PASSES):
+                columns = slice(i * FEATURES, (i + 1) * FEATURES)
+                prepare_unit(
+                    [
+                        w_words[r][:, f, i * WORDS_PASS : (i + 1) * WORDS_PASS]
+                        for f in range(FEATURE_TILES)
+                    ],
+                    codes[:, columns],
+                    scales[:, columns],
+                    vector_helps=(i % 2 == 0),
+                )
+
+        sums = {}
+        biased = {}
+
+        def multiply(first, last):
+            for n in range(first, last):
+                w, g = divmod(n, PASSES)
+                r, i = divmod(n, ROUND_PASSES)
+                for t in range(TOKEN_TILES):
+                    if g == 0:
+                        acc = sum_pool.tile([P, FEATURES], F32)
+                        sums[(w, t)] = acc
+                    tokens = slice((g * TOKEN_TILES + t) * P, (g * TOKEN_TILES + t + 1) * P)
+                    features = slice(i * FEATURES, (i + 1) * FEATURES)
+                    nc.tensor.matmul_mx(
+                        out=sums[(w, t)][:],
+                        lhsT=x_codes[:, tokens].bitcast(FP8X4),
+                        lhsT_scale=x_scales[:, tokens],
+                        rhs=w_codes[r][:, features].bitcast(FP8X4),
+                        rhs_scale=w_scales[r][:, features],
+                        start=(g == 0),
+                        stop=(g == PASSES - 1),
+                    )
+                if g == PASSES - 1:
+                    for t in range(TOKEN_TILES):
+                        y = result_pool.tile([P, FEATURES], F32)
+                        nc.vector.tensor_tensor(
+                            out=y[:],
+                            in0=sums[(w, t)][:],
+                            in1=bias_all[:, w * FEATURES : (w + 1) * FEATURES],
+                            op=ADD,
+                        )
+                        biased[(w, t)] = y
+
+        def store(queue, w, t, y):
+            queue.dma_start(
+                out=outs[w][t].rearrange("h s d -> s h d"),
+                in_=y[:].rearrange("p (h d) -> p h d", h=HEADS),
+            )
+
+        def normalise_and_store(w):
+            square_sums = []
+            for t in range(TOKEN_TILES):
+                squares = result_pool.tile([P, FEATURES], F32)
+                square_sum = small_pool.tile([P, 1], F32)
+                nc.scalar.activation(
+                    out=squares[:], in_=biased[(w, t)][:], func=SQUARE, accum_out=square_sum[:]
+                )
+                square_sums.append(square_sum)
+            floored_sums = []
+            for t in range(TOKEN_TILES):
+                floored = small_pool.tile([P, 1], F32)
+                nc.vector.tensor_scalar_max(floored[:], square_sums[t][:], 1e-24)
+                floored_sums.append(floored)
+            norms = []
+            for t in range(TOKEN_TILES):
+                norm = small_pool.tile([P, 1], F32)
+                nc.scalar.activation(out=norm[:], in_=floored_sums[t][:], func=SQRT)
+                norms.append(norm)
+            inverse_norms = []
+            for t in range(TOKEN_TILES):
+                inverse = small_pool.tile([P, 1], F32)
+                nc.vector.reciprocal(inverse[:], norms[t][:])
+                inverse_norms.append(inverse)
+            for t in range(TOKEN_TILES):
+                y = biased[(w, t)]
+                nc.scalar.activation(out=y[:], in_=y[:], func=COPY, scale=inverse_norms[t][:])
+                store(nc.scalar, w, t, y)
+
+        for r in range(ROUNDS):
+            w, c = divmod(r, ROUNDS_PER_WEIGHT)
+            if w == 0:
+                prepare_x(c)
+            prepare_w(r)
+            if r + LOADS_AHEAD < ROUNDS:
+                load_w(r + LOADS_AHEAD)
+            if w > 0 and c == 1:
+                normalise_and_store(w - 1)
+            multiply(max(0, r * ROUND_PASSES - LAG), (r + 1) * ROUND_PASSES - LAG)
+        multiply(ROUNDS * ROUND_PASSES - LAG, ROUNDS * ROUND_PASSES)
+        store(nc.sync, WEIGHTS - 1, 0, biased[(WEIGHTS - 1, 0)])
+        store(nc.scalar, WEIGHTS - 1, 1, biased[(WEIGHTS - 1, 1)])

@@ -57,6 +57,32 @@ def tile_knnxlmultiheadsattention_pa_k_kernel(
         sum_pool = ctx.enter_context(tc.psum_pool(name="sums", bufs=3))
         bank_pool = ctx.enter_context(tc.psum_pool(name="banks", bufs=5))
 
+        bias_line = const.tile([1, WEIGHTS * FEATURES], BF16)
+        for w in range(WEIGHTS):
+            nc.sync.dma_start(
+                out=bias_line[0:1, w * FEATURES : (w + 1) * FEATURES],
+                in_=biases[w].rearrange("(o n) -> o n", o=1),
+            )
+        bias_rows = const.tile([P, WEIGHTS * FEATURES], BF16)
+        nc.vector.memset(bias_rows[:], 0.0)
+        nc.vector.tensor_copy(out=bias_rows[0:1, :], in_=bias_line[:])
+        ones = const.tile([P, P], BF16)
+        nc.vector.memset(ones[:], 1.0)
+        bias_all = const.tile([P, WEIGHTS * FEATURES], F32)
+        for w in range(WEIGHTS):
+            columns = slice(w * FEATURES, (w + 1) * FEATURES)
+            bank = bank_pool.tile([P, 2, BANK_COLUMNS], F32)
+            spread = bank[:].rearrange("p u n -> p (u n)")
+            nc.tensor.matmul(spread, lhsT=ones[:], rhs=bias_rows[:, columns], start=True, stop=True)
+            nc.vector.tensor_copy(out=bias_all[:, columns], in_=spread)
+
+        identity = const.tile([P, P], F32)
+        make_identity(nc, identity[:])
+
+        warm = const.tile([P, 1], F32)
+        nc.vector.memset(warm[:], 1.0)
+        nc.scalar.activation(out=warm[:], in_=warm[:], func=SQRT)
+
         x_by_token = x.rearrange("b s k -> s b k")
         x_words = {}
         w_words = {}
@@ -84,28 +110,6 @@ def tile_knnxlmultiheadsattention_pa_k_kernel(
             if r < ROUNDS_PER_WEIGHT:
                 load_x(r)
             load_w(r)
-
-        identity = const.tile([P, P], F32)
-        make_identity(nc, identity[:])
-
-        warm = const.tile([P, 1], F32)
-        nc.vector.memset(warm[:], 1.0)
-        nc.scalar.activation(out=warm[:], in_=warm[:], func=SQRT)
-
-        bias_rows = const.tile([P, WEIGHTS * FEATURES], BF16)
-        nc.vector.memset(bias_rows[:], 0.0)
-        ones = const.tile([P, P], BF16)
-        nc.vector.memset(ones[:], 1.0)
-        bias_all = const.tile([P, WEIGHTS * FEATURES], F32)
-        for w in range(WEIGHTS):
-            columns = slice(w * FEATURES, (w + 1) * FEATURES)
-            nc.scalar.dma_start(
-                out=bias_rows[0:1, columns], in_=biases[w].rearrange("(o n) -> o n", o=1)
-            )
-            bank = bank_pool.tile([P, 2, BANK_COLUMNS], F32)
-            spread = bank[:].rearrange("p u n -> p (u n)")
-            nc.tensor.matmul(spread, lhsT=ones[:], rhs=bias_rows[:, columns], start=True, stop=True)
-            nc.vector.tensor_copy(out=bias_all[:, columns], in_=spread)
 
         x_codes = const.tile([P, PASSES * TOKEN_TILES * P], U32, align_bytes=64)
         x_scales = const.tile([P, PASSES * TOKEN_TILES * P], U8, align_bytes=64)

@@ -24,12 +24,16 @@ FEATURE_TILES = FEATURES // P
 HEADS = 8
 WEIGHTS = 3
 
-ROUND_PASSES = 4
-K_ROUND = ROUND_PASSES * K_PASS
+LOAD_PASSES = 4
+K_LOAD = LOAD_PASSES * K_PASS
+LOADS_PER_WEIGHT = PASSES // LOAD_PASSES
+LOADS = WEIGHTS * LOADS_PER_WEIGHT
+LOADS_AHEAD = 5
+
+ROUND_PASSES = 2
 ROUNDS_PER_WEIGHT = PASSES // ROUND_PASSES
 ROUNDS = WEIGHTS * ROUNDS_PER_WEIGHT
 LAG = 2
-LOADS_AHEAD = 5
 
 UNIT_COLUMNS = 512
 BANK_COLUMNS = UNIT_COLUMNS // 2
@@ -48,10 +52,10 @@ def tile_knnxlmultiheadsattention_pa_k_kernel(
     with ExitStack() as ctx:
         ctx.enter_context(tc.manual_schedule())
         const = ctx.enter_context(tc.tile_pool(name="const", bufs=1))
-        x_raw_pool = ctx.enter_context(tc.tile_pool(name="x_raw", bufs=ROUNDS_PER_WEIGHT))
+        x_raw_pool = ctx.enter_context(tc.tile_pool(name="x_raw", bufs=LOADS_PER_WEIGHT))
         w_raw_pool = ctx.enter_context(tc.tile_pool(name="w_raw", bufs=LOADS_AHEAD))
         grouped_pool = ctx.enter_context(tc.tile_pool(name="grouped", bufs=4))
-        w_mx_pool = ctx.enter_context(tc.tile_pool(name="w_mx", bufs=3))
+        w_mx_pool = ctx.enter_context(tc.tile_pool(name="w_mx", bufs=4))
         result_pool = ctx.enter_context(tc.tile_pool(name="result", bufs=4))
         small_pool = ctx.enter_context(tc.tile_pool(name="small", bufs=4))
         sum_pool = ctx.enter_context(tc.psum_pool(name="sums", bufs=3))
@@ -88,28 +92,28 @@ def tile_knnxlmultiheadsattention_pa_k_kernel(
         w_words = {}
 
         def load_x(c):
-            x_raw = x_raw_pool.tile([P, TOKEN_TILES * K_ROUND], BF16)
+            x_raw = x_raw_pool.tile([P, TOKEN_TILES * K_LOAD], BF16)
             nc.sync.dma_start(
                 out=x_raw[:].rearrange("p (t k) -> p t k", t=TOKEN_TILES),
-                in_=x_by_token[:, :, c * K_ROUND : (c + 1) * K_ROUND],
+                in_=x_by_token[:, :, c * K_LOAD : (c + 1) * K_LOAD],
             )
             x_words[c] = x_raw[:].bitcast(F32).rearrange("p (t w) -> p t w", t=TOKEN_TILES)
 
-        def load_w(r):
-            w, c = divmod(r, ROUNDS_PER_WEIGHT)
-            w_raw = w_raw_pool.tile([P, FEATURE_TILES * K_ROUND], BF16)
+        def load_w(l):
+            w, c = divmod(l, LOADS_PER_WEIGHT)
+            w_raw = w_raw_pool.tile([P, FEATURE_TILES * K_LOAD], BF16)
             nc.sync.dma_start(
                 out=w_raw[:].rearrange("p (f k) -> p f k", f=FEATURE_TILES),
                 in_=weights[w].rearrange("(f p) k -> p f k", p=P)[
-                    :, :, c * K_ROUND : (c + 1) * K_ROUND
+                    :, :, c * K_LOAD : (c + 1) * K_LOAD
                 ],
             )
-            w_words[r] = w_raw[:].bitcast(F32).rearrange("p (f w) -> p f w", f=FEATURE_TILES)
+            w_words[l] = w_raw[:].bitcast(F32).rearrange("p (f w) -> p f w", f=FEATURE_TILES)
 
-        for r in range(LOADS_AHEAD):
-            if r < ROUNDS_PER_WEIGHT:
-                load_x(r)
-            load_w(r)
+        for l in range(LOADS_AHEAD):
+            if l < LOADS_PER_WEIGHT:
+                load_x(l)
+            load_w(l)
 
         x_codes = const.tile([P, PASSES * TOKEN_TILES * P], U32, align_bytes=64)
         x_scales = const.tile([P, PASSES * TOKEN_TILES * P], U8, align_bytes=64)
@@ -134,9 +138,9 @@ def tile_knnxlmultiheadsattention_pa_k_kernel(
                     nc.scalar.copy(out=side_by_side, in_=alternately)
             nc.vector.quantize_mx(out=codes.bitcast(FP8X4), scales=scales, in_=grouped[:])
 
-        def prepare_x(c):
-            for i in range(0, ROUND_PASSES, 2):
-                g = c * ROUND_PASSES + i
+        def prepare_x(first, last):
+            for g in range(first, last, 2):
+                c, i = divmod(g, LOAD_PASSES)
                 columns = slice(g * TOKEN_TILES * P, (g + 2) * TOKEN_TILES * P)
                 prepare_unit(
                     [
@@ -146,7 +150,7 @@ def tile_knnxlmultiheadsattention_pa_k_kernel(
                     ],
                     x_codes[:, columns],
                     x_scales[:, columns],
-                    vector_helps=(i % 4 == 0),
+                    vector_helps=(g % 4 == 0),
                 )
 
         w_codes = {}
@@ -158,10 +162,11 @@ def tile_knnxlmultiheadsattention_pa_k_kernel(
             w_codes[r] = codes
             w_scales[r] = scales
             for i in range(ROUND_PASSES):
+                l, j = divmod(r * ROUND_PASSES + i, LOAD_PASSES)
                 columns = slice(i * FEATURES, (i + 1) * FEATURES)
                 prepare_unit(
                     [
-                        w_words[r][:, f, i * WORDS_PASS : (i + 1) * WORDS_PASS]
+                        w_words[l][:, f, j * WORDS_PASS : (j + 1) * WORDS_PASS]
                         for f in range(FEATURE_TILES)
                     ],
                     codes[:, columns],
@@ -240,10 +245,11 @@ def tile_knnxlmultiheadsattention_pa_k_kernel(
         for r in range(ROUNDS):
             w, c = divmod(r, ROUNDS_PER_WEIGHT)
             if w == 0:
-                prepare_x(c)
+                prepare_x(r * ROUND_PASSES, (r + 1) * ROUND_PASSES)
             prepare_w(r)
-            if r + LOADS_AHEAD < ROUNDS:
-                load_w(r + LOADS_AHEAD)
+            l, passes_left = divmod((r + 1) * ROUND_PASSES, LOAD_PASSES)
+            if passes_left == 0 and l - 1 + LOADS_AHEAD < LOADS:
+                load_w(l - 1 + LOADS_AHEAD)
             if w > 0 and c == 1:
                 normalise_and_store(w - 1)
             multiply(max(0, r * ROUND_PASSES - LAG), (r + 1) * ROUND_PASSES - LAG)

@@ -24,11 +24,11 @@ FEATURE_TILES = FEATURES // P
 HEADS = 8
 WEIGHTS = 3
 
-LOAD_PASSES = 4
+LOAD_PASSES = 2
 K_LOAD = LOAD_PASSES * K_PASS
 LOADS_PER_WEIGHT = PASSES // LOAD_PASSES
 LOADS = WEIGHTS * LOADS_PER_WEIGHT
-LOADS_AHEAD = 5
+LOADS_AHEAD = 10
 
 ROUND_PASSES = 2
 ROUNDS_PER_WEIGHT = PASSES // ROUND_PASSES
@@ -213,34 +213,53 @@ def tile_knnxlmultiheadsattention_pa_k_kernel(
                 in_=y[:].rearrange("p (h d) -> p h d", h=HEADS),
             )
 
-        def normalise_and_store(w):
-            square_sums = []
-            for t in range(TOKEN_TILES):
-                squares = result_pool.tile([P, FEATURES], F32)
-                square_sum = small_pool.tile([P, 1], F32)
-                nc.scalar.activation(
-                    out=squares[:], in_=biased[(w, t)][:], func=SQUARE, accum_out=square_sum[:]
-                )
-                square_sums.append(square_sum)
-            floored_sums = []
-            for t in range(TOKEN_TILES):
-                floored = small_pool.tile([P, 1], F32)
-                nc.vector.tensor_scalar_max(floored[:], square_sums[t][:], 1e-24)
-                floored_sums.append(floored)
-            norms = []
-            for t in range(TOKEN_TILES):
-                norm = small_pool.tile([P, 1], F32)
-                nc.scalar.activation(out=norm[:], in_=floored_sums[t][:], func=SQRT)
-                norms.append(norm)
-            inverse_norms = []
-            for t in range(TOKEN_TILES):
-                inverse = small_pool.tile([P, 1], F32)
-                nc.vector.reciprocal(inverse[:], norms[t][:])
-                inverse_norms.append(inverse)
-            for t in range(TOKEN_TILES):
-                y = biased[(w, t)]
-                nc.scalar.activation(out=y[:], in_=y[:], func=COPY, scale=inverse_norms[t][:])
-                store(nc.scalar, w, t, y)
+        square_sums = {}
+        norms = {}
+        inverse_norms = {}
+
+        def square_sum(w, t):
+            if t == 0:
+                sums_of_squares = small_pool.tile([P, TOKEN_TILES], F32)
+                square_sums[w] = sums_of_squares
+            squares = result_pool.tile([P, FEATURES], F32)
+            nc.scalar.activation(
+                out=squares[:],
+                in_=biased[(w, t)][:],
+                func=SQUARE,
+                accum_out=square_sums[w][:, t : t + 1],
+            )
+
+        def norm(w):
+            both = small_pool.tile([P, TOKEN_TILES], F32)
+            nc.scalar.activation(out=both[:], in_=square_sums[w][:], func=SQRT)
+            norms[w] = both
+
+        def inverse_norm(w):
+            floored = small_pool.tile([P, TOKEN_TILES], F32)
+            nc.vector.tensor_scalar_max(floored[:], norms[w][:], 1e-12)
+            inverse = small_pool.tile([P, TOKEN_TILES], F32)
+            nc.vector.reciprocal(inverse[:], floored[:])
+            inverse_norms[w] = inverse
+
+        def scale_and_store(w, t):
+            y = biased[(w, t)]
+            nc.scalar.activation(
+                out=y[:], in_=y[:], func=COPY, scale=inverse_norms[w][:, t : t + 1]
+            )
+            store(nc.scalar, w, t, y)
+
+        def finish_step(w, c):
+            if c == 1:
+                square_sum(w, 0)
+            elif c == 2:
+                square_sum(w, 1)
+                norm(w)
+            elif c == 3:
+                inverse_norm(w)
+            elif c == 4:
+                scale_and_store(w, 0)
+            elif c == 5:
+                scale_and_store(w, 1)
 
         for r in range(ROUNDS):
             w, c = divmod(r, ROUNDS_PER_WEIGHT)
@@ -250,8 +269,8 @@ def tile_knnxlmultiheadsattention_pa_k_kernel(
             l, passes_left = divmod((r + 1) * ROUND_PASSES, LOAD_PASSES)
             if passes_left == 0 and l - 1 + LOADS_AHEAD < LOADS:
                 load_w(l - 1 + LOADS_AHEAD)
-            if w > 0 and c == 1:
-                normalise_and_store(w - 1)
+            if w > 0:
+                finish_step(w - 1, c)
             multiply(max(0, r * ROUND_PASSES - LAG), (r + 1) * ROUND_PASSES - LAG)
         multiply(ROUNDS * ROUND_PASSES - LAG, ROUNDS * ROUND_PASSES)
         store(nc.sync, WEIGHTS - 1, 0, biased[(WEIGHTS - 1, 0)])

@@ -30,10 +30,10 @@ LOADS_PER_WEIGHT = PASSES // LOAD_PASSES
 LOADS = WEIGHTS * LOADS_PER_WEIGHT
 LOADS_AHEAD = 10
 
-ROUND_PASSES = 2
-ROUNDS_PER_WEIGHT = PASSES // ROUND_PASSES
-ROUNDS = WEIGHTS * ROUNDS_PER_WEIGHT
-LAG = 2
+ROUND_SIZES = (2,) * (PASSES // 2) + (4,) * ((WEIGHTS - 1) * PASSES // 4)
+LONGEST_ROUND = max(ROUND_SIZES)
+SUM_BANKS = 2
+TRANSPOSE_BANKS = 6
 
 UNIT_COLUMNS = 512
 BANK_COLUMNS = UNIT_COLUMNS // 2
@@ -55,11 +55,11 @@ def tile_knnxlmultiheadsattention_pa_k_kernel(
         x_raw_pool = ctx.enter_context(tc.tile_pool(name="x_raw", bufs=LOADS_PER_WEIGHT))
         w_raw_pool = ctx.enter_context(tc.tile_pool(name="w_raw", bufs=LOADS_AHEAD))
         grouped_pool = ctx.enter_context(tc.tile_pool(name="grouped", bufs=4))
-        w_mx_pool = ctx.enter_context(tc.tile_pool(name="w_mx", bufs=4))
+        w_mx_pool = ctx.enter_context(tc.tile_pool(name="w_mx", bufs=2 * LONGEST_ROUND + 2))
         result_pool = ctx.enter_context(tc.tile_pool(name="result", bufs=4))
         small_pool = ctx.enter_context(tc.tile_pool(name="small", bufs=4))
-        sum_pool = ctx.enter_context(tc.psum_pool(name="sums", bufs=3))
-        bank_pool = ctx.enter_context(tc.psum_pool(name="banks", bufs=5))
+        sum_pool = ctx.enter_context(tc.psum_pool(name="sums", bufs=SUM_BANKS))
+        bank_pool = ctx.enter_context(tc.psum_pool(name="banks", bufs=TRANSPOSE_BANKS))
 
         bias_line = const.tile([1, WEIGHTS * FEATURES], BF16)
         for w in range(WEIGHTS):
@@ -118,6 +118,13 @@ def tile_knnxlmultiheadsattention_pa_k_kernel(
         x_codes = const.tile([P, PASSES * TOKEN_TILES * P], U32, align_bytes=64)
         x_scales = const.tile([P, PASSES * TOKEN_TILES * P], U8, align_bytes=64)
 
+        waiting = []
+
+        def quantise_waiting():
+            for codes, scales, grouped in waiting:
+                nc.vector.quantize_mx(out=codes.bitcast(FP8X4), scales=scales, in_=grouped[:])
+            waiting.clear()
+
         def prepare_unit(sources, codes, scales, vector_helps):
             grouped = grouped_pool.tile([P, 4 * UNIT_COLUMNS], BF16, align_bytes=64)
             grouped_words = grouped[:].bitcast(F32).rearrange("p (n u) -> p n u", u=2)
@@ -136,7 +143,8 @@ def tile_knnxlmultiheadsattention_pa_k_kernel(
                     nc.vector.tensor_copy(out=side_by_side, in_=alternately)
                 else:
                     nc.scalar.copy(out=side_by_side, in_=alternately)
-            nc.vector.quantize_mx(out=codes.bitcast(FP8X4), scales=scales, in_=grouped[:])
+            quantise_waiting()
+            waiting.append((codes, scales, grouped))
 
         def prepare_x(first, last):
             for g in range(first, last, 2):
@@ -156,62 +164,62 @@ def tile_knnxlmultiheadsattention_pa_k_kernel(
         w_codes = {}
         w_scales = {}
 
-        def prepare_w(r):
-            codes = w_mx_pool.tile([P, ROUND_PASSES * FEATURES], U32, align_bytes=64)
-            scales = w_mx_pool.tile([P, ROUND_PASSES * FEATURES], U8, align_bytes=64)
-            w_codes[r] = codes
-            w_scales[r] = scales
-            for i in range(ROUND_PASSES):
-                l, j = divmod(r * ROUND_PASSES + i, LOAD_PASSES)
-                columns = slice(i * FEATURES, (i + 1) * FEATURES)
-                prepare_unit(
-                    [
-                        w_words[l][:, f, j * WORDS_PASS : (j + 1) * WORDS_PASS]
-                        for f in range(FEATURE_TILES)
-                    ],
-                    codes[:, columns],
-                    scales[:, columns],
-                    vector_helps=(i % 2 == 0),
-                )
+        def prepare_w(n):
+            codes = w_mx_pool.tile([P, FEATURES], U32, align_bytes=64)
+            scales = w_mx_pool.tile([P, FEATURES], U8, align_bytes=64)
+            w_codes[n] = codes
+            w_scales[n] = scales
+            l, j = divmod(n, LOAD_PASSES)
+            prepare_unit(
+                [
+                    w_words[l][:, f, j * WORDS_PASS : (j + 1) * WORDS_PASS]
+                    for f in range(FEATURE_TILES)
+                ],
+                codes[:],
+                scales[:],
+                vector_helps=(n % 2 == 0),
+            )
 
         sums = {}
         biased = {}
-
-        def multiply(first, last):
-            for n in range(first, last):
-                w, g = divmod(n, PASSES)
-                r, i = divmod(n, ROUND_PASSES)
-                for t in range(TOKEN_TILES):
-                    if g == 0:
-                        acc = sum_pool.tile([P, FEATURES], F32)
-                        sums[(w, t)] = acc
-                    tokens = slice((g * TOKEN_TILES + t) * P, (g * TOKEN_TILES + t + 1) * P)
-                    features = slice(i * FEATURES, (i + 1) * FEATURES)
-                    nc.tensor.matmul_mx(
-                        out=sums[(w, t)][:],
-                        lhsT=x_codes[:, tokens].bitcast(FP8X4),
-                        lhsT_scale=x_scales[:, tokens],
-                        rhs=w_codes[r][:, features].bitcast(FP8X4),
-                        rhs_scale=w_scales[r][:, features],
-                        start=(g == 0),
-                        stop=(g == PASSES - 1),
-                    )
-                if g == PASSES - 1:
-                    for t in range(TOKEN_TILES):
-                        y = result_pool.tile([P, FEATURES], F32)
-                        nc.vector.tensor_tensor(
-                            out=y[:],
-                            in0=sums[(w, t)][:],
-                            in1=bias_all[:, w * FEATURES : (w + 1) * FEATURES],
-                            op=ADD,
-                        )
-                        biased[(w, t)] = y
 
         def store(queue, w, t, y):
             queue.dma_start(
                 out=outs[w][t].rearrange("h s d -> s h d"),
                 in_=y[:].rearrange("p (h d) -> p h d", h=HEADS),
             )
+
+        def multiply(first, last, tile_by_tile=False):
+            if tile_by_tile:
+                order = [(n, t) for t in range(TOKEN_TILES) for n in range(first, last)]
+            else:
+                order = [(n, t) for n in range(first, last) for t in range(TOKEN_TILES)]
+            for n, t in order:
+                w, g = divmod(n, PASSES)
+                if g == 0:
+                    acc = sum_pool.tile([P, FEATURES], F32)
+                    sums[(w, t)] = acc
+                tokens = slice((g * TOKEN_TILES + t) * P, (g * TOKEN_TILES + t + 1) * P)
+                nc.tensor.matmul_mx(
+                    out=sums[(w, t)][:],
+                    lhsT=x_codes[:, tokens].bitcast(FP8X4),
+                    lhsT_scale=x_scales[:, tokens],
+                    rhs=w_codes[n][:].bitcast(FP8X4),
+                    rhs_scale=w_scales[n][:],
+                    start=(g == 0),
+                    stop=(g == PASSES - 1),
+                )
+                if g == PASSES - 1:
+                    y = result_pool.tile([P, FEATURES], F32)
+                    nc.vector.tensor_tensor(
+                        out=y[:],
+                        in0=sums[(w, t)][:],
+                        in1=bias_all[:, w * FEATURES : (w + 1) * FEATURES],
+                        op=ADD,
+                    )
+                    biased[(w, t)] = y
+                    if w == WEIGHTS - 1:
+                        store(nc.sync if t == 0 else nc.scalar, w, t, y)
 
         square_sums = {}
         norms = {}
@@ -248,30 +256,34 @@ def tile_knnxlmultiheadsattention_pa_k_kernel(
             )
             store(nc.scalar, w, t, y)
 
-        def finish_step(w, c):
-            if c == 1:
+        def finish_step(w, g):
+            if g == LONGEST_ROUND:
                 square_sum(w, 0)
-            elif c == 2:
+            elif g == LONGEST_ROUND + 2:
                 square_sum(w, 1)
                 norm(w)
-            elif c == 3:
+            elif g == LONGEST_ROUND + 4:
                 inverse_norm(w)
-            elif c == 4:
+            elif g == LONGEST_ROUND + 6:
                 scale_and_store(w, 0)
-            elif c == 5:
+            elif g == LONGEST_ROUND + 8:
                 scale_and_store(w, 1)
 
-        for r in range(ROUNDS):
-            w, c = divmod(r, ROUNDS_PER_WEIGHT)
-            if w == 0:
-                prepare_x(r * ROUND_PASSES, (r + 1) * ROUND_PASSES)
-            prepare_w(r)
-            l, passes_left = divmod((r + 1) * ROUND_PASSES, LOAD_PASSES)
-            if passes_left == 0 and l - 1 + LOADS_AHEAD < LOADS:
-                load_w(l - 1 + LOADS_AHEAD)
-            if w > 0:
-                finish_step(w - 1, c)
-            multiply(max(0, r * ROUND_PASSES - LAG), (r + 1) * ROUND_PASSES - LAG)
-        multiply(ROUNDS * ROUND_PASSES - LAG, ROUNDS * ROUND_PASSES)
-        store(nc.sync, WEIGHTS - 1, 0, biased[(WEIGHTS - 1, 0)])
-        store(nc.scalar, WEIGHTS - 1, 1, biased[(WEIGHTS - 1, 1)])
+        first = 0
+        before = (0, 0)
+        for size in ROUND_SIZES:
+            for n in range(first, first + size):
+                w, g = divmod(n, PASSES)
+                if w == 0 and g % 2 == 0:
+                    prepare_x(g, g + 2)
+                prepare_w(n)
+                l, passes_left = divmod(n + 1, LOAD_PASSES)
+                if passes_left == 0 and l - 1 + LOADS_AHEAD < LOADS:
+                    load_w(l - 1 + LOADS_AHEAD)
+                if w > 0:
+                    finish_step(w - 1, g)
+            quantise_waiting()
+            multiply(before[0], before[1])
+            before = (first, first + size)
+            first += size
+        multiply(before[0], before[1], tile_by_tile=True)

@@ -254,7 +254,7 @@ def tile_knnxlmultiheadsattention_pa_k_kernel(
             nc.scalar.activation(
                 out=y[:], in_=y[:], func=COPY, scale=inverse_norms[w][:, t : t + 1]
             )
-            store(nc.scalar, w, t, y)
+            store(nc.sync, w, t, y)
 
         def finish_step(w, g):
             if g == LONGEST_ROUND:
@@ -264,9 +264,9 @@ def tile_knnxlmultiheadsattention_pa_k_kernel(
                 norm(w)
             elif g == LONGEST_ROUND + 4:
                 inverse_norm(w)
-            elif g == LONGEST_ROUND + 6:
+            elif g == LONGEST_ROUND + (8 if w == 0 else 6):
                 scale_and_store(w, 0)
-            elif g == LONGEST_ROUND + 8:
+            elif g == LONGEST_ROUND + (9 if w == 0 else 7):
                 scale_and_store(w, 1)
 
         first = 0
@@ -280,6 +280,7 @@ def tile_knnxlmultiheadsattention_pa_k_kernel(
                 l, passes_left = divmod(n + 1, LOAD_PASSES)
                 if passes_left == 0 and l - 1 + LOADS_AHEAD < LOADS:
                     load_w(l - 1 + LOADS_AHEAD)
+                    last_load_behind_pass = n
                 if w > 0:
                     finish_step(w - 1, g)
             quantise_waiting()
@@ -287,3 +288,4 @@ def tile_knnxlmultiheadsattention_pa_k_kernel(
             before = (first, first + size)
             first += size
         multiply(before[0], before[1], tile_by_tile=True)
+        assert last_load_behind_pass < PASSES + LONGEST_ROUND + 8

@@ -111,9 +111,9 @@ def tile_knnxlmultiheadsattention_pa_k_kernel(
             w_words[l] = w_raw[:].bitcast(F32).rearrange("p (f w) -> p f w", f=FEATURE_TILES)
 
         for l in range(LOADS_AHEAD):
+            load_w(l)
             if l < LOADS_PER_WEIGHT:
                 load_x(l)
-            load_w(l)
 
         x_codes = const.tile([P, PASSES * TOKEN_TILES * P], U32, align_bytes=64)
         x_scales = const.tile([P, PASSES * TOKEN_TILES * P], U8, align_bytes=64)
@@ -183,10 +183,18 @@ def tile_knnxlmultiheadsattention_pa_k_kernel(
         sums = {}
         biased = {}
 
-        def store(queue, w, t, y):
+        def store(queue, w, t, y, first_head=0, last_head=HEADS):
             queue.dma_start(
-                out=outs[w][t].rearrange("h s d -> s h d"),
-                in_=y[:].rearrange("p (h d) -> p h d", h=HEADS),
+                out=outs[w][t].rearrange("h s d -> s h d")[:, first_head:last_head, :],
+                in_=y[:].rearrange("p (h d) -> p h d", h=HEADS)[:, first_head:last_head, :],
+            )
+
+        def add_bias(w, t, first, last):
+            nc.vector.tensor_tensor(
+                out=biased[(w, t)][:, first:last],
+                in0=sums[(w, t)][:, first:last],
+                in1=bias_all[:, w * FEATURES + first : w * FEATURES + last],
+                op=ADD,
             )
 
         def multiply(first, last, tile_by_tile=False):
@@ -211,15 +219,14 @@ def tile_knnxlmultiheadsattention_pa_k_kernel(
                 )
                 if g == PASSES - 1:
                     y = result_pool.tile([P, FEATURES], F32)
-                    nc.vector.tensor_tensor(
-                        out=y[:],
-                        in0=sums[(w, t)][:],
-                        in1=bias_all[:, w * FEATURES : (w + 1) * FEATURES],
-                        op=ADD,
-                    )
                     biased[(w, t)] = y
-                    if w == WEIGHTS - 1:
-                        store(nc.sync if t == 0 else nc.scalar, w, t, y)
+                    if w < WEIGHTS - 1:
+                        add_bias(w, t, 0, FEATURES)
+                    else:
+                        add_bias(w, t, 0, FEATURES // 2)
+                        store(nc.sync, w, t, y, 0, HEADS // 2)
+                        add_bias(w, t, FEATURES // 2, FEATURES)
+                        store(nc.scalar, w, t, y, HEADS // 2, HEADS)
 
         square_sums = {}
         norms = {}
@@ -257,16 +264,13 @@ def tile_knnxlmultiheadsattention_pa_k_kernel(
             store(nc.sync, w, t, y)
 
         def finish_step(w, g):
-            if g == LONGEST_ROUND:
+            if g == 2 * LONGEST_ROUND - 1:
                 square_sum(w, 0)
-            elif g == LONGEST_ROUND + 2:
                 square_sum(w, 1)
                 norm(w)
-            elif g == LONGEST_ROUND + 4:
+            elif g == 3 * LONGEST_ROUND - 1:
                 inverse_norm(w)
-            elif g == LONGEST_ROUND + (8 if w == 0 else 6):
                 scale_and_store(w, 0)
-            elif g == LONGEST_ROUND + (9 if w == 0 else 7):
                 scale_and_store(w, 1)
 
         first = 0
@@ -274,9 +278,9 @@ def tile_knnxlmultiheadsattention_pa_k_kernel(
         for size in ROUND_SIZES:
             for n in range(first, first + size):
                 w, g = divmod(n, PASSES)
-                if w == 0 and g % 2 == 0:
-                    prepare_x(g, g + 2)
                 prepare_w(n)
+                if w == 0 and g % 2 == 1:
+                    prepare_x(g - 1, g + 1)
                 l, passes_left = divmod(n + 1, LOAD_PASSES)
                 if passes_left == 0 and l - 1 + LOADS_AHEAD < LOADS:
                     load_w(l - 1 + LOADS_AHEAD)
@@ -288,4 +292,4 @@ def tile_knnxlmultiheadsattention_pa_k_kernel(
             before = (first, first + size)
             first += size
         multiply(before[0], before[1], tile_by_tile=True)
-        assert last_load_behind_pass < PASSES + LONGEST_ROUND + 8
+        assert last_load_behind_pass <= PASSES + 3 * LONGEST_ROUND - 1

@@ -115,8 +115,8 @@ def tile_knnxlmultiheadsattention_pa_k_kernel(
             if l < LOADS_PER_WEIGHT:
                 load_x(l)
 
-        x_codes = const.tile([P, PASSES * TOKEN_TILES * P], U32, align_bytes=64)
-        x_scales = const.tile([P, PASSES * TOKEN_TILES * P], U8, align_bytes=64)
+        x_codes = const.tile([P, PASSES * TOKEN_TILES * P], U32, align_bytes=256)
+        x_scales = const.tile([P, PASSES * TOKEN_TILES * P], U8, align_bytes=256)
 
         waiting = []
 
@@ -126,7 +126,7 @@ def tile_knnxlmultiheadsattention_pa_k_kernel(
             waiting.clear()
 
         def prepare_unit(sources, codes, scales, vector_helps):
-            grouped = grouped_pool.tile([P, 4 * UNIT_COLUMNS], BF16, align_bytes=64)
+            grouped = grouped_pool.tile([P, 4 * UNIT_COLUMNS], BF16, align_bytes=256)
             grouped_words = grouped[:].bitcast(F32).rearrange("p (n u) -> p n u", u=2)
             for half in range(2):
                 bank = bank_pool.tile([P, 2, BANK_COLUMNS], F32)
@@ -165,8 +165,8 @@ def tile_knnxlmultiheadsattention_pa_k_kernel(
         w_scales = {}
 
         def prepare_w(n):
-            codes = w_mx_pool.tile([P, FEATURES], U32, align_bytes=64)
-            scales = w_mx_pool.tile([P, FEATURES], U8, align_bytes=64)
+            codes = w_mx_pool.tile([P, FEATURES], U32, align_bytes=256)
+            scales = w_mx_pool.tile([P, FEATURES], U8, align_bytes=256)
             w_codes[n] = codes
             w_scales[n] = scales
             l, j = divmod(n, LOAD_PASSES)

@@ -80,7 +80,7 @@ def tile_knnxlmultiheadsattention_pa_k_kernel(
             nc.tensor.matmul(spread, lhsT=ones[:], rhs=bias_rows[:, columns], start=True, stop=True)
             nc.vector.tensor_copy(out=bias_all[:, columns], in_=spread)
 
-        identity = const.tile([P, P], F32)
+        identity = const.tile([P, P], F32, align_bytes=256)
         make_identity(nc, identity[:])
 
         warm = const.tile([P, 1], F32)
@@ -92,7 +92,7 @@ def tile_knnxlmultiheadsattention_pa_k_kernel(
         w_words = {}
 
         def load_x(c):
-            x_raw = x_raw_pool.tile([P, TOKEN_TILES * K_LOAD], BF16)
+            x_raw = x_raw_pool.tile([P, TOKEN_TILES * K_LOAD], BF16, align_bytes=256)
             nc.sync.dma_start(
                 out=x_raw[:].rearrange("p (t k) -> p t k", t=TOKEN_TILES),
                 in_=x_by_token[:, :, c * K_LOAD : (c + 1) * K_LOAD],
@@ -101,7 +101,7 @@ def tile_knnxlmultiheadsattention_pa_k_kernel(
 
         def load_w(l):
             w, c = divmod(l, LOADS_PER_WEIGHT)
-            w_raw = w_raw_pool.tile([P, FEATURE_TILES * K_LOAD], BF16)
+            w_raw = w_raw_pool.tile([P, FEATURE_TILES * K_LOAD], BF16, align_bytes=256)
             nc.sync.dma_start(
                 out=w_raw[:].rearrange("p (f k) -> p f k", f=FEATURE_TILES),
                 in_=weights[w].rearrange("(f p) k -> p f k", p=P)[

@@ -72,7 +72,7 @@ def tile_knnxlmultiheadsattention_pa_k_kernel(
         nc.vector.tensor_copy(out=bias_rows[0:1, :], in_=bias_line[:])
         ones = const.tile([P, P], BF16)
         nc.vector.memset(ones[:], 1.0)
-        bias_all = const.tile([P, WEIGHTS * FEATURES], F32)
+        bias_all = const.tile([P, WEIGHTS * FEATURES], F32, align_bytes=1024)
         for w in range(WEIGHTS):
             columns = slice(w * FEATURES, (w + 1) * FEATURES)
             bank = bank_pool.tile([P, 2, BANK_COLUMNS], F32)
@@ -80,7 +80,7 @@ def tile_knnxlmultiheadsattention_pa_k_kernel(
             nc.tensor.matmul(spread, lhsT=ones[:], rhs=bias_rows[:, columns], start=True, stop=True)
             nc.vector.tensor_copy(out=bias_all[:, columns], in_=spread)
 
-        identity = const.tile([P, P], F32, align_bytes=256)
+        identity = const.tile([P, P], F32, align_bytes=1024)
         make_identity(nc, identity[:])
 
         warm = const.tile([P, 1], F32)
@@ -92,7 +92,7 @@ def tile_knnxlmultiheadsattention_pa_k_kernel(
         w_words = {}
 
         def load_x(c):
-            x_raw = x_raw_pool.tile([P, TOKEN_TILES * K_LOAD], BF16, align_bytes=256)
+            x_raw = x_raw_pool.tile([P, TOKEN_TILES * K_LOAD], BF16, align_bytes=1024)
             nc.sync.dma_start(
                 out=x_raw[:].rearrange("p (t k) -> p t k", t=TOKEN_TILES),
                 in_=x_by_token[:, :, c * K_LOAD : (c + 1) * K_LOAD],
@@ -101,7 +101,7 @@ def tile_knnxlmultiheadsattention_pa_k_kernel(
 
         def load_w(l):
             w, c = divmod(l, LOADS_PER_WEIGHT)
-            w_raw = w_raw_pool.tile([P, FEATURE_TILES * K_LOAD], BF16, align_bytes=256)
+            w_raw = w_raw_pool.tile([P, FEATURE_TILES * K_LOAD], BF16, align_bytes=1024)
             nc.sync.dma_start(
                 out=w_raw[:].rearrange("p (f k) -> p f k", f=FEATURE_TILES),
                 in_=weights[w].rearrange("(f p) k -> p f k", p=P)[
@@ -115,8 +115,8 @@ def tile_knnxlmultiheadsattention_pa_k_kernel(
             if l < LOADS_PER_WEIGHT:
                 load_x(l)
 
-        x_codes = const.tile([P, PASSES * TOKEN_TILES * P], U32, align_bytes=256)
-        x_scales = const.tile([P, PASSES * TOKEN_TILES * P], U8, align_bytes=256)
+        x_codes = const.tile([P, PASSES * TOKEN_TILES * P], U32, align_bytes=1024)
+        x_scales = const.tile([P, PASSES * TOKEN_TILES * P], U8, align_bytes=1024)
 
         waiting = []
 
@@ -126,7 +126,7 @@ def tile_knnxlmultiheadsattention_pa_k_kernel(
             waiting.clear()
 
         def prepare_unit(sources, codes, scales, vector_helps):
-            grouped = grouped_pool.tile([P, 4 * UNIT_COLUMNS], BF16, align_bytes=256)
+            grouped = grouped_pool.tile([P, 4 * UNIT_COLUMNS], BF16, align_bytes=1024)
             grouped_words = grouped[:].bitcast(F32).rearrange("p (n u) -> p n u", u=2)
             for half in range(2):
                 bank = bank_pool.tile([P, 2, BANK_COLUMNS], F32)
@@ -165,8 +165,8 @@ def tile_knnxlmultiheadsattention_pa_k_kernel(
         w_scales = {}
 
         def prepare_w(n):
-            codes = w_mx_pool.tile([P, FEATURES], U32, align_bytes=256)
-            scales = w_mx_pool.tile([P, FEATURES], U8, align_bytes=256)
+            codes = w_mx_pool.tile([P, FEATURES], U32, align_bytes=1024)
+            scales = w_mx_pool.tile([P, FEATURES], U8, align_bytes=1024)
             w_codes[n] = codes
             w_scales[n] = scales
             l, j = divmod(n, LOAD_PASSES)
@@ -218,7 +218,7 @@ def tile_knnxlmultiheadsattention_pa_k_kernel(
                     stop=(g == PASSES - 1),
                 )
                 if g == PASSES - 1:
-                    y = result_pool.tile([P, FEATURES], F32)
+                    y = result_pool.tile([P, FEATURES], F32, align_bytes=1024)
                     biased[(w, t)] = y
                     if w < WEIGHTS - 1:
                         add_bias(w, t, 0, FEATURES)
@@ -236,7 +236,7 @@ def tile_knnxlmultiheadsattention_pa_k_kernel(
             if t == 0:
                 sums_of_squares = small_pool.tile([P, TOKEN_TILES], F32)
                 square_sums[w] = sums_of_squares
-            squares = result_pool.tile([P, FEATURES], F32)
+            squares = result_pool.tile([P, FEATURES], F32, align_bytes=1024)
             nc.scalar.activation(
                 out=squares[:],
                 in_=biased[(w, t)][:],

from contextlib import ExitStack

import concourse.mybir as mybir
from concourse.masks import make_identity

F32 = mybir.dt.float32
BF16 = mybir.dt.bfloat16
U32 = mybir.dt.uint32
U8 = mybir.dt.uint8
FP8X4 = mybir.dt.float8_e4m3fn_x4
ADD = mybir.AluOpType.add
SQUARE = mybir.ActivationFunctionType.Square
SQRT = mybir.ActivationFunctionType.Sqrt
COPY = mybir.ActivationFunctionType.Copy

P = 128
K = 8192
K_PASS = 512
WORDS_PASS = K_PASS // 2
PASSES = K // K_PASS
TOKEN_TILES = 2
FEATURES = 512
FEATURE_TILES = FEATURES // P
HEADS = 8
WEIGHTS = 3

LOAD_PASSES = 2
K_LOAD = LOAD_PASSES * K_PASS
LOADS_PER_WEIGHT = PASSES // LOAD_PASSES
LOADS = WEIGHTS * LOADS_PER_WEIGHT
LOADS_AHEAD = 10

ROUND_SIZES = (2,) * (PASSES // 2) + (4,) * ((WEIGHTS - 1) * PASSES // 4)
LONGEST_ROUND = max(ROUND_SIZES)
SUM_BANKS = 2
TRANSPOSE_BANKS = 6

UNIT_COLUMNS = 512
BANK_COLUMNS = UNIT_COLUMNS // 2

FLOPS = 2 * TOKEN_TILES * P * WEIGHTS * FEATURES * K


def tile_knnxlmultiheadsattention_pa_k_kernel(
    tc, x, wq, bq, wk, bk, wv, bv, out_q, out_k, out_v
):
    nc = tc.nc
    weights = [wq, wk, wv]
    biases = [bq, bk, bv]
    outs = [out_q, out_k, out_v]

    with ExitStack() as ctx:
        ctx.enter_context(tc.manual_schedule())
        const = ctx.enter_context(tc.tile_pool(name="const", bufs=1))
        x_raw_pool = ctx.enter_context(tc.tile_pool(name="x_raw", bufs=LOADS_PER_WEIGHT))
        w_raw_pool = ctx.enter_context(tc.tile_pool(name="w_raw", bufs=LOADS_AHEAD))
        grouped_pool = ctx.enter_context(tc.tile_pool(name="grouped", bufs=4))
        w_mx_pool = ctx.enter_context(tc.tile_pool(name="w_mx", bufs=2 * LONGEST_ROUND + 2))
        result_pool = ctx.enter_context(tc.tile_pool(name="result", bufs=4))
        small_pool = ctx.enter_context(tc.tile_pool(name="small", bufs=4))
        sum_pool = ctx.enter_context(tc.psum_pool(name="sums", bufs=SUM_BANKS))
        bank_pool = ctx.enter_context(tc.psum_pool(name="banks", bufs=TRANSPOSE_BANKS))

        bias_line = const.tile([1, WEIGHTS * FEATURES], BF16)
        for w in range(WEIGHTS):
            nc.sync.dma_start(
                out=bias_line[0:1, w * FEATURES : (w + 1) * FEATURES],
                in_=biases[w].rearrange("(o n) -> o n", o=1),
            )
        bias_rows = const.tile([P, WEIGHTS * FEATURES], BF16)
        nc.vector.memset(bias_rows[:], 0.0)
        nc.vector.tensor_copy(out=bias_rows[0:1, :], in_=bias_line[:])
        ones = const.tile([P, P], BF16)
        nc.vector.memset(ones[:], 1.0)
        bias_all = const.tile([P, WEIGHTS * FEATURES], F32, align_bytes=1024)
        for w in range(WEIGHTS):
            columns = slice(w * FEATURES, (w + 1) * FEATURES)
            bank = bank_pool.tile([P, 2, BANK_COLUMNS], F32)
            spread = bank[:].rearrange("p u n -> p (u n)")
            nc.tensor.matmul(spread, lhsT=ones[:], rhs=bias_rows[:, columns], start=True, stop=True)
            nc.vector.tensor_copy(out=bias_all[:, columns], in_=spread)

        identity = const.tile([P, P], F32, align_bytes=1024)
        make_identity(nc, identity[:])

        warm = const.tile([P, 1], F32)
        nc.vector.memset(warm[:], 1.0)
        nc.scalar.activation(out=warm[:], in_=warm[:], func=SQRT)

        x_by_token = x.rearrange("b s k -> s b k")
        x_words = {}
        w_words = {}

        def load_x(c):
            x_raw = x_raw_pool.tile([P, TOKEN_TILES * K_LOAD], BF16, align_bytes=1024)
            nc.sync.dma_start(
                out=x_raw[:].rearrange("p (t k) -> p t k", t=TOKEN_TILES),
                in_=x_by_token[:, :, c * K_LOAD : (c + 1) * K_LOAD],
            )
            x_words[c] = x_raw[:].bitcast(F32).rearrange("p (t w) -> p t w", t=TOKEN_TILES)

        def load_w(l):
            w, c = divmod(l, LOADS_PER_WEIGHT)
            w_raw = w_raw_pool.tile([P, FEATURE_TILES * K_LOAD], BF16, align_bytes=1024)
            nc.sync.dma_start(
                out=w_raw[:].rearrange("p (f k) -> p f k", f=FEATURE_TILES),
                in_=weights[w].rearrange("(f p) k -> p f k", p=P)[
                    :, :, c * K_LOAD : (c + 1) * K_LOAD
                ],
            )
            w_words[l] = w_raw[:].bitcast(F32).rearrange("p (f w) -> p f w", f=FEATURE_TILES)

        for l in range(LOADS_AHEAD):
            load_w(l)
            if l < LOADS_PER_WEIGHT:
                load_x(l)

        x_codes = const.tile([P, PASSES * TOKEN_TILES * P], U32, align_bytes=1024)
        x_scales = const.tile([P, PASSES * TOKEN_TILES * P], U8, align_bytes=1024)

        waiting = []

        def quantise_waiting():
            for codes, scales, grouped in waiting:
                nc.vector.quantize_mx(out=codes.bitcast(FP8X4), scales=scales, in_=grouped[:])
            waiting.clear()

        def prepare_unit(sources, codes, scales, vector_helps):
            grouped = grouped_pool.tile([P, 4 * UNIT_COLUMNS], BF16, align_bytes=1024)
            grouped_words = grouped[:].bitcast(F32).rearrange("p (n u) -> p n u", u=2)
            for half in range(2):
                bank = bank_pool.tile([P, 2, BANK_COLUMNS], F32)
                for j in range(2):
                    for u in range(2):
                        nc.tensor.transpose(
                            bank[:, u, j * P : (j + 1) * P],
                            sources[2 * half + j][:, u * P : (u + 1) * P],
                            identity[:],
                        )
                side_by_side = grouped_words[:, half * BANK_COLUMNS : (half + 1) * BANK_COLUMNS, :]
                alternately = bank[:].rearrange("p u n -> p n u")
                if vector_helps and half == 0:
                    nc.vector.tensor_copy(out=side_by_side, in_=alternately)
                else:
                    nc.scalar.copy(out=side_by_side, in_=alternately)
            quantise_waiting()
            waiting.append((codes, scales, grouped))

        def prepare_x(first, last):
            for g in range(first, last, 2):
                c, i = divmod(g, LOAD_PASSES)
                columns = slice(g * TOKEN_TILES * P, (g + 2) * TOKEN_TILES * P)
                prepare_unit(
                    [
                        x_words[c][:, t, (i + d) * WORDS_PASS : (i + d + 1) * WORDS_PASS]
                        for d in range(2)
                        for t in range(TOKEN_TILES)
                    ],
                    x_codes[:, columns],
                    x_scales[:, columns],
                    vector_helps=(g % 4 == 0),
                )

        w_codes = {}
        w_scales = {}

        def prepare_w(n):
            codes = w_mx_pool.tile([P, FEATURES], U32, align_bytes=1024)
            scales = w_mx_pool.tile([P, FEATURES], U8, align_bytes=1024)
            w_codes[n] = codes
            w_scales[n] = scales
            l, j = divmod(n, LOAD_PASSES)
            prepare_unit(
                [
                    w_words[l][:, f, j * WORDS_PASS : (j + 1) * WORDS_PASS]
                    for f in range(FEATURE_TILES)
                ],
                codes[:],
                scales[:],
                vector_helps=(n % 2 == 0),
            )

        sums = {}
        biased = {}

        def store(queue, w, t, y, first_head=0, last_head=HEADS):
            queue.dma_start(
                out=outs[w][t].rearrange("h s d -> s h d")[:, first_head:last_head, :],
                in_=y[:].rearrange("p (h d) -> p h d", h=HEADS)[:, first_head:last_head, :],
            )

        def add_bias(w, t, first, last):
            nc.vector.tensor_tensor(
                out=biased[(w, t)][:, first:last],
                in0=sums[(w, t)][:, first:last],
                in1=bias_all[:, w * FEATURES + first : w * FEATURES + last],
                op=ADD,
            )

        def multiply(first, last, tile_by_tile=False):
            if tile_by_tile:
                order = [(n, t) for t in range(TOKEN_TILES) for n in range(first, last)]
            else:
                order = [(n, t) for n in range(first, last) for t in range(TOKEN_TILES)]
            for n, t in order:
                w, g = divmod(n, PASSES)
                if g == 0:
                    acc = sum_pool.tile([P, FEATURES], F32)
                    sums[(w, t)] = acc
                tokens = slice((g * TOKEN_TILES + t) * P, (g * TOKEN_TILES + t + 1) * P)
                nc.tensor.matmul_mx(
                    out=sums[(w, t)][:],
                    lhsT=x_codes[:, tokens].bitcast(FP8X4),
                    lhsT_scale=x_scales[:, tokens],
                    rhs=w_codes[n][:].bitcast(FP8X4),
                    rhs_scale=w_scales[n][:],
                    start=(g == 0),
                    stop=(g == PASSES - 1),
                )
                if g == PASSES - 1:
                    y = result_pool.tile([P, FEATURES], F32, align_bytes=1024)
                    biased[(w, t)] = y
                    if w < WEIGHTS - 1:
                        add_bias(w, t, 0, FEATURES)
                    else:
                        add_bias(w, t, 0, FEATURES // 2)
                        store(nc.sync, w, t, y, 0, HEADS // 2)
                        add_bias(w, t, FEATURES // 2, FEATURES)
                        store(nc.scalar, w, t, y, HEADS // 2, HEADS)

        square_sums = {}
        norms = {}
        inverse_norms = {}

        def square_sum(w, t):
            if t == 0:
                sums_of_squares = small_pool.tile([P, TOKEN_TILES], F32)
                square_sums[w] = sums_of_squares
            squares = result_pool.tile([P, FEATURES], F32, align_bytes=1024)
            nc.scalar.activation(
                out=squares[:],
                in_=biased[(w, t)][:],
                func=SQUARE,
                accum_out=square_sums[w][:, t : t + 1],
            )

        def norm(w):
            both = small_pool.tile([P, TOKEN_TILES], F32)
            nc.scalar.activation(out=both[:], in_=square_sums[w][:], func=SQRT)
            norms[w] = both

        def inverse_norm(w):
            floored = small_pool.tile([P, TOKEN_TILES], F32)
            nc.vector.tensor_scalar_max(floored[:], norms[w][:], 1e-12)
            inverse = small_pool.tile([P, TOKEN_TILES], F32)
            nc.vector.reciprocal(inverse[:], floored[:])
            inverse_norms[w] = inverse

        def scale_and_store(w, t):
            y = biased[(w, t)]
            nc.scalar.activation(
                out=y[:], in_=y[:], func=COPY, scale=inverse_norms[w][:, t : t + 1]
            )
            store(nc.sync, w, t, y)

        def finish_step(w, g):
            if g == 2 * LONGEST_ROUND - 1:
                square_sum(w, 0)
                square_sum(w, 1)
                norm(w)
            elif g == 3 * LONGEST_ROUND - 1:
                inverse_norm(w)
                scale_and_store(w, 0)
                scale_and_store(w, 1)

        first = 0
        before = (0, 0)
        for size in ROUND_SIZES:
            for n in range(first, first + size):
                w, g = divmod(n, PASSES)
                prepare_w(n)
                if w == 0 and g % 2 == 1:
                    prepare_x(g - 1, g + 1)
                l, passes_left = divmod(n + 1, LOAD_PASSES)
                if passes_left == 0 and l - 1 + LOADS_AHEAD < LOADS:
                    load_w(l - 1 + LOADS_AHEAD)
                    last_load_behind_pass = n
                if w > 0:
                    finish_step(w - 1, g)
            quantise_waiting()
            multiply(before[0], before[1])
            before = (first, first + size)
            first += size
        multiply(before[0], before[1], tile_by_tile=True)
        assert last_load_behind_pass <= PASSES + 3 * LONGEST_ROUND - 1
